import numpy as np
import ml_dtypes


def mxq(x, axis, fmt="e4m3"):
    dtype, down = {"e4m3": (ml_dtypes.float8_e4m3fn, 7), "e5m2": (ml_dtypes.float8_e5m2, 14)}[fmt]
    v = np.moveaxis(np.asarray(x, np.float32).astype(ml_dtypes.bfloat16).astype(np.float64), axis, -1)
    blocks = v.reshape(v.shape[:-1] + (-1, 32))
    amax = np.abs(blocks).max(-1, keepdims=True)
    byte = np.maximum(np.where(amax > 0, np.frexp(amax)[1] - 1 + 127, 0) - down, 1)
    scale = np.exp2(byte - 127.0)
    codes = (blocks / scale).astype(np.float32).astype(dtype).astype(np.float64)
    return np.moveaxis((codes * scale).reshape(v.shape), -1, axis)


WIDE = False


def mx_kscale(k):
    if not WIDE:
        return np.ones(k)
    levels = np.array([30, -30])
    if k % 512:
        return np.exp2(np.random.permutation(np.resize(levels, k // 32))).repeat(32)
    a = np.empty((k // 512, 16))
    for p in range(k // 512):
        a[p, :8] = np.random.permutation(np.resize(levels, 8))
        for g in range(8):
            far = levels[np.abs(levels - a[p, g]) >= 10]
            a[p, g + 8] = far[np.random.randint(len(far))]
    return np.exp2(a.ravel()).repeat(32)


BF16 = ml_dtypes.bfloat16


def bf(x):
    return np.asarray(x, np.float32).astype(BF16)


def f64(x):
    return np.asarray(x).astype(np.float64)


B, S, H, HO, E = 4, 128, 1024, 1024, 8


def kahan_sum_last(x):
    s = np.zeros_like(x[..., 0])
    c = np.zeros_like(s)
    for i in range(x.shape[-1]):
        y = x[..., i] - c
        t = s + y
        c = (t - s) - y
        s = t
    return s


def setup_inputs():
    s = mx_kscale(H)
    return {"hidden_states": bf(np.random.standard_normal((B, S, H)) * s),
            "op_logits": bf(np.random.standard_normal((B, S, E)) * 1.3),
            "We": bf(np.random.standard_normal((E, H, HO)) / np.sqrt(H) / s[None, :, None]),
            "be": bf(np.random.standard_normal((E, HO)) * 0.3)}


def reference(hidden_states, op_logits, We, be):
    l = f64(op_logits)
    ex = np.exp(l - l.max(-1, keepdims=True))
    op_w = ex / ex.sum(-1, keepdims=True)
    prod = mxq(f64(hidden_states), 2, "e5m2")[:, None] @ mxq(f64(We), 1, "e4m3")[None]
    expert_out = prod.transpose(0, 2, 1, 3) + f64(be)
    weighted = expert_out * op_w[:, :, :, None]
    return kahan_sum_last(np.moveaxis(weighted, 2, -1))

@@ -1,0 +1,270 @@
+from contextlib import ExitStack
+
+import concourse.mybir as mybir
+from concourse.masks import make_identity
+
+TOKENS, H, HO, E = 512, 1024, 1024, 8
+FLOPS = 2 * E * TOKENS * H * HO
+
+F32 = mybir.dt.float32
+BF16 = mybir.dt.bfloat16
+U32 = mybir.dt.uint32
+U8 = mybir.dt.uint8
+E4M3X4 = mybir.dt.float8_e4m3fn_x4
+E5M2X4 = mybir.dt.float8_e5m2_x4
+ALU = mybir.AluOpType
+ACT = mybir.ActivationFunctionType
+AX = mybir.AxisListType
+
+P = 128
+PACK = 4
+K_PASS = P * PACK
+PASSES = H // K_PASS
+TILES = TOKENS // P
+N = 512
+HALVES = HO // N
+UNITS = E * HALVES
+BANKS = 8
+
+HEAD_UNITS = 5
+HEAD_V = 384
+BODY_V = 64
+TAIL_UNITS = 2
+G_COLS = 0
+G_FROM = 3
+BIAS_FROM = 3
+RUN = 4
+
+
+def tile_enhancedmathematicalreasoning_pa_kernel(tc, hidden_states, op_logits, We, be, out):
+    nc = tc.nc
+    x_hbm = hidden_states.rearrange("b s k -> (b s) k").rearrange("(p j) k -> p j k", j=TILES)
+    logits_hbm = op_logits.rearrange("b s e -> (b s) e").rearrange("(p j) e -> p j e", j=TILES)
+    out_hbm = out.rearrange("b s n -> (b s) n").rearrange("(p j) n -> p j n", j=TILES)
+
+    with ExitStack() as ctx:
+        keep = ctx.enter_context(tc.tile_pool(name="keep", bufs=1))
+        stream = ctx.enter_context(tc.tile_pool(name="stream", bufs=3))
+        psum = ctx.enter_context(tc.psum_pool(name="psum", bufs=BANKS))
+        ctx.enter_context(tc.manual_schedule())
+
+        logits = keep.tile([P, TILES, E], BF16)
+        nc.sync.dma_start(out=logits[:], in_=logits_hbm)
+        bias_rows = keep.tile([P, HO], BF16)
+        nc.sync.dma_start(out=bias_rows[0:E, :], in_=be)
+        x_raw = []
+        for pair in range(TILES // 2):
+            x_pair = keep.tile([P, 2, H], BF16, name="x_pair%d" % pair)
+            nc.sync.dma_start(out=x_pair[:], in_=x_hbm[:, 2 * pair : 2 * pair + 2, :])
+            x_raw.extend([x_pair[:, 0, :], x_pair[:, 1, :]])
+        w_raw = {}
+        for h in range(HALVES):
+            for g in range(PASSES):
+                piece = keep.tile([P, PACK, N], BF16, name="w0_%d_%d" % (h, g))
+                rows = We[0, g * K_PASS : (g + 1) * K_PASS, h * N : (h + 1) * N]
+                nc.sync.dma_start(out=piece[:], in_=rows.rearrange("(p t) n -> p t n", t=PACK))
+                w_raw[(h, g)] = piece[:]
+        for e in range(1, E):
+            for g in range(PASSES):
+                piece = keep.tile([P, PACK, HO], BF16, name="w%d_%d" % (e, g))
+                rows = We[e, g * K_PASS : (g + 1) * K_PASS, :]
+                nc.sync.dma_start(out=piece[:], in_=rows.rearrange("(p t) n -> p t n", t=PACK))
+                for h in range(HALVES):
+                    w_raw[(HALVES * e + h, g)] = piece[:, :, h * N : (h + 1) * N]
+
+        ident = keep.tile([P, P], F32)
+        make_identity(nc, ident[:])
+        gate = keep.tile([P, (TILES - 1) * E + P], F32)
+        nc.gpsimd.memset(gate[:], 0.0)
+        bias32 = keep.tile([P, HO], F32)
+        nc.gpsimd.memset(bias32[:], 0.0)
+
+        top = keep.tile([P, TILES], F32)
+        nc.vector.tensor_reduce(out=top[:], in_=logits[:], axis=AX.X, op=ALU.max)
+        shifted = keep.tile([P, TILES, E], F32)
+        nc.vector.tensor_tensor(
+            out=shifted[:], in0=logits[:], in1=top[:].unsqueeze(2).to_broadcast([P, TILES, E]), op=ALU.subtract
+        )
+        ex = keep.tile([P, TILES, E], F32)
+        nc.scalar.activation(out=ex[:], in_=shifted[:], func=ACT.Exp)
+        total = keep.tile([P, TILES], F32)
+        nc.vector.tensor_reduce(out=total[:], in_=ex[:], axis=AX.X, op=ALU.add)
+        inv = keep.tile([P, TILES], F32)
+        nc.vector.reciprocal(out=inv[:], in_=total[:])
+        nc.vector.tensor_tensor(
+            out=gate[:, 0 : TILES * E].rearrange("p (j e) -> p j e", e=E),
+            in0=ex[:],
+            in1=inv[:].unsqueeze(2).to_broadcast([P, TILES, E]),
+            op=ALU.mult,
+        )
+        nc.scalar.copy(out=bias32[0:E, :], in_=bias_rows[0:E, :])
+
+        x_codes = {}
+        x_scales = {}
+
+        def quantize_x(j):
+            words = x_raw[j].bitcast(F32)
+            bank = psum.tile([P, 2 * PASSES, P], F32, tag="bank", name="x_bank")
+            for g in range(PASSES):
+                for u in range(2):
+                    nc.tensor.transpose(bank[:, 2 * g + u, :], words[:, 256 * g + u : 256 * (g + 1) : 2], ident[:])
+            grouped = keep.tile([P, PASSES, P, 2], F32, name="x_grouped%d" % j, align_bytes=64)
+            nc.scalar.copy(out=grouped[:], in_=bank[:].rearrange("p (g u) r -> p g r u", u=2))
+            codes = keep.tile([P, PASSES * P], U32, name="x_codes%d" % j, align_bytes=64)
+            scales = keep.tile([P, PASSES * P], U8, name="x_scales%d" % j, align_bytes=64)
+            nc.vector.quantize_mx(
+                out=codes[:].bitcast(E5M2X4),
+                scales=scales[:],
+                in_=grouped[:].rearrange("p g r u -> p (g r u)").bitcast(BF16),
+            )
+            x_codes[j] = codes
+            x_scales[j] = scales
+
+        def g_cols(unit, g):
+            return G_COLS if (g == PASSES - 1 and unit >= G_FROM) else 0
+
+        def v_cols(unit, g):
+            if unit < HEAD_UNITS:
+                return min(HEAD_V, N - g_cols(unit, g))
+            if unit >= UNITS - TAIL_UNITS or g > 0:
+                return 0
+            return BODY_V
+
+        staged = {}
+        staged_g = {}
+
+        def stage_tile(unit, g):
+            if (unit, g) not in staged:
+                staged[(unit, g)] = stream.tile([P, N, PACK], BF16, tag="stage", name="stage", bufs=6, align_bytes=64)
+            return staged[(unit, g)]
+
+        def views(dst, src):
+            return dst.rearrange("p (c i) t -> p c t i", i=RUN), src.rearrange("p t (c i) -> p c t i", i=RUN)
+
+        def copy_v(unit, g):
+            n = v_cols(unit, g)
+            if n:
+                dst, src = views(stage_tile(unit, g)[:, 0:n, :], w_raw[(unit, g)][:, :, 0:n])
+                nc.vector.tensor_copy(out=dst, in_=src)
+
+        def copy_s(unit, g):
+            n0, n1 = v_cols(unit, g), N - g_cols(unit, g)
+            if n1 > n0:
+                dst, src = views(stage_tile(unit, g)[:, n0:n1, :], w_raw[(unit, g)][:, :, n0:n1])
+                nc.scalar.copy(out=dst, in_=src)
+
+        def copy_g(unit):
+            n = g_cols(unit, PASSES - 1)
+            if n:
+                tile_g = keep.tile([P, n, PACK], BF16, tag="stage_g", name="stage_g", align_bytes=64)
+                staged_g[unit] = tile_g
+                dst, src = views(tile_g[:], w_raw[(unit, PASSES - 1)][:, :, N - n : N])
+                nc.gpsimd.tensor_copy(out=dst, in_=src)
+
+        w_codes = {}
+        w_scales = {}
+
+        def quantize_w(unit, g):
+            if g == 0:
+                w_codes[unit] = stream.tile([P, PASSES, N], U32, tag="w_codes", name="w_codes", align_bytes=64)
+                w_scales[unit] = stream.tile([P, PASSES, N], U8, tag="w_scales", name="w_scales", align_bytes=64)
+            n1 = N - g_cols(unit, g)
+            nc.vector.quantize_mx(
+                out=w_codes[unit][:, g, 0:n1].bitcast(E4M3X4),
+                scales=w_scales[unit][:, g, 0:n1],
+                in_=staged[(unit, g)][:, 0:n1, :].rearrange("p n t -> p (n t)"),
+            )
+            if n1 < N:
+                nc.vector.quantize_mx(
+                    out=w_codes[unit][:, g, n1:N].bitcast(E4M3X4),
+                    scales=w_scales[unit][:, g, n1:N],
+                    in_=staged_g[unit][:].rearrange("p n t -> p (n t)"),
+                )
+
+        acc = {}
+        for j in range(TILES):
+            for h in range(HALVES):
+                acc[(j, h)] = keep.tile([P, N], F32, name="acc%d_%d" % (j, h))
+
+        jobs = []
+        drained = [0]
+
+        def drain_oldest():
+            bank, kind, unit, j, h = jobs[drained[0]]
+            drained[0] += 1
+            dst = acc[(j, h)]
+            if kind == "bias":
+                nc.vector.tensor_tensor(out=dst[:], in0=bank[:], in1=dst[:], op=ALU.add)
+                return
+            e = unit // HALVES
+            w_col = gate[:, j * E + e : j * E + e + 1]
+            if e == 0:
+                nc.scalar.activation(out=dst[:], in_=bank[:], func=ACT.Copy, scale=w_col)
+            else:
+                nc.vector.scalar_tensor_tensor(
+                    out=dst[:], in0=bank[:], scalar=w_col, in1=dst[:], op0=ALU.mult, op1=ALU.add
+                )
+            if e == E - 1:
+                nc.sync.dma_start(out=out_hbm[:, j, h * N : (h + 1) * N], in_=dst[:])
+
+        def take_bank():
+            if len(jobs) - drained[0] == BANKS:
+                drain_oldest()
+            return psum.tile([P, N], F32, tag="bank", name="bank")
+
+        def multiply(unit):
+            for j in range(TILES):
+                bank = take_bank()
+                for g in range(PASSES):
+                    nc.tensor.matmul_mx(
+                        out=bank[:],
+                        lhsT=x_codes[j][:, g * P : (g + 1) * P].bitcast(E5M2X4),
+                        lhsT_scale=x_scales[j][:, g * P : (g + 1) * P],
+                        rhs=w_codes[unit][:, g, :].bitcast(E4M3X4),
+                        rhs_scale=w_scales[unit][:, g, :],
+                        start=(g == 0),
+                        stop=(g == PASSES - 1),
+                    )
+                jobs.append((bank, "mx", unit, j, unit % HALVES))
+
+        def bias_product(j, h):
+            bank = take_bank()
+            nc.tensor.matmul(bank[:], lhsT=gate_t[:, j, :], rhs=bias32[:, h * N : (h + 1) * N], start=True, stop=True)
+            jobs.append((bank, "bias", 0, j, h))
+
+        quantize_x(0)
+        quantize_x(1)
+        gate_bank = psum.tile([P, TILES, P], F32, tag="bank", name="gate_bank")
+        for j in range(TILES):
+            nc.tensor.transpose(gate_bank[:, j, :], gate[:, j * E : j * E + P], ident[:])
+        quantize_x(2)
+        copy_v(0, 0)
+        quantize_x(3)
+        gate_t = keep.tile([P, TILES, P], F32)
+        nc.scalar.copy(out=gate_t[:], in_=gate_bank[:])
+        copy_s(0, 0)
+        copy_v(0, 1)
+        copy_s(0, 1)
+        quantize_w(0, 0)
+
+        for step in range(1, UNITS + 2):
+            if step < UNITS:
+                copy_v(step, 0)
+            if step <= UNITS:
+                if step > 1:
+                    quantize_w(step - 1, 0)
+                quantize_w(step - 1, 1)
+            if step < UNITS:
+                copy_g(step)
+                copy_s(step, 0)
+                copy_v(step, 1)
+            older = len(jobs)
+            if step <= UNITS:
+                multiply(step - 1)
+            i = step - BIAS_FROM
+            if 0 <= i < TILES * HALVES:
+                bias_product(i // HALVES, step % HALVES)
+            for job in range(drained[0], older):
+                drain_oldest()
+            if step < UNITS:
+                copy_s(step, 1)

@@ -26,14 +26,21 @@ HALVES = HO // N
 UNITS = E * HALVES
 BANKS = 8
 
-HEAD_UNITS = 5
-HEAD_V = 384
-BODY_V = 64
-TAIL_UNITS = 2
-G_COLS = 0
-G_FROM = 3
-BIAS_FROM = 3
+MERGED = 2
+LAST_MERGED = (7, 6)
+HEAD_UNITS = 2
+HEAD_V = 512
+BODY_V = 512
+STEP_V = 64
+HEAD_BIAS = 1
+HEAD_V1 = 896
+TAIL_V = 512
+TAIL_UNITS = 1
+LEAD_S = 0
+BIAS_STEPS = (4, 6)
+W_FIRST = 0
 RUN = 4
+PARTS = 3
 
 
 def tile_enhancedmathematicalreasoning_pa_kernel(tc, hidden_states, op_logits, We, be, out):
@@ -45,39 +52,50 @@ def tile_enhancedmathematicalreasoning_pa_kernel(tc, hidden_states, op_logits, W
     with ExitStack() as ctx:
         keep = ctx.enter_context(tc.tile_pool(name="keep", bufs=1))
         stream = ctx.enter_context(tc.tile_pool(name="stream", bufs=3))
-        psum = ctx.enter_context(tc.psum_pool(name="psum", bufs=BANKS))
+        psum = ctx.enter_context(tc.psum_pool(name="psum", bufs=1))
         ctx.enter_context(tc.manual_schedule())
 
         logits = keep.tile([P, TILES, E], BF16)
         nc.sync.dma_start(out=logits[:], in_=logits_hbm)
         bias_rows = keep.tile([P, HO], BF16)
-        nc.sync.dma_start(out=bias_rows[0:E, :], in_=be)
-        x_raw = []
-        for pair in range(TILES // 2):
-            x_pair = keep.tile([P, 2, H], BF16, name="x_pair%d" % pair)
-            nc.sync.dma_start(out=x_pair[:], in_=x_hbm[:, 2 * pair : 2 * pair + 2, :])
-            x_raw.extend([x_pair[:, 0, :], x_pair[:, 1, :]])
+        nc.vector.memset(bias_rows[:], 0.0)
+        for part in range(PARTS):
+            nc.scalar.dma_start(out=bias_rows[part * E : (part + 1) * E, :], in_=be)
+        x_raw = {}
         w_raw = {}
-        for h in range(HALVES):
+
+        def load_x(j):
+            x_tile = keep.tile([P, H], BF16, name="x_tile%d" % j)
+            nc.sync.dma_start(out=x_tile[:], in_=x_hbm[:, j, :])
+            x_raw[j] = x_tile[:]
+
+        def load_w(unit, g):
+            h, e = divmod(unit, E)
+            piece = keep.tile([P, PACK, N], BF16, name="w%d_%d" % (unit, g))
+            rows = We[e, g * K_PASS : (g + 1) * K_PASS, h * N : (h + 1) * N]
+            nc.sync.dma_start(out=piece[:], in_=rows.rearrange("(p t) n -> p t n", t=PACK))
+            w_raw[(unit, g)] = piece[:]
+
+        if W_FIRST == 0:
+            load_x(0)
+        load_w(0, 0)
+        if W_FIRST == 1:
+            load_x(0)
+        load_x(1)
+        load_w(0, 1)
+        load_x(2)
+        load_x(3)
+        for unit in range(1, UNITS):
             for g in range(PASSES):
-                piece = keep.tile([P, PACK, N], BF16, name="w0_%d_%d" % (h, g))
-                rows = We[0, g * K_PASS : (g + 1) * K_PASS, h * N : (h + 1) * N]
-                nc.sync.dma_start(out=piece[:], in_=rows.rearrange("(p t) n -> p t n", t=PACK))
-                w_raw[(h, g)] = piece[:]
-        for e in range(1, E):
-            for g in range(PASSES):
-                piece = keep.tile([P, PACK, HO], BF16, name="w%d_%d" % (e, g))
-                rows = We[e, g * K_PASS : (g + 1) * K_PASS, :]
-                nc.sync.dma_start(out=piece[:], in_=rows.rearrange("(p t) n -> p t n", t=PACK))
-                for h in range(HALVES):
-                    w_raw[(HALVES * e + h, g)] = piece[:, :, h * N : (h + 1) * N]
+                load_w(unit, g)
 
         ident = keep.tile([P, P], F32)
         make_identity(nc, ident[:])
-        gate = keep.tile([P, (TILES - 1) * E + P], F32)
-        nc.gpsimd.memset(gate[:], 0.0)
-        bias32 = keep.tile([P, HO], F32)
-        nc.gpsimd.memset(bias32[:], 0.0)
+        ident16 = keep.tile([P, P], BF16)
+        make_identity(nc, ident16[:])
+        gate = keep.tile([P, TILES * E], F32)
+        parts = keep.tile([P, (TILES - 1) * PARTS * E + P], BF16)
+        nc.gpsimd.memset(parts[:], 0.0)
 
         top = keep.tile([P, TILES], F32)
         nc.vector.tensor_reduce(out=top[:], in_=logits[:], axis=AX.X, op=ALU.max)
@@ -97,19 +115,27 @@ def tile_enhancedmathematicalreasoning_pa_kernel(tc, hidden_states, op_logits, W
             in1=inv[:].unsqueeze(2).to_broadcast([P, TILES, E]),
             op=ALU.mult,
         )
-        nc.scalar.copy(out=bias32[0:E, :], in_=bias_rows[0:E, :])
+        part_view = parts[:, 0 : TILES * PARTS * E].rearrange("p (j q e) -> p j q e", q=PARTS, e=E)
+        gate_view = gate[:].rearrange("p (j e) -> p j e", e=E)
+        rest = keep.tile([P, TILES, E], F32)
 
         x_codes = {}
         x_scales = {}
 
-        def quantize_x(j):
+        x_grouped = {}
+
+        def turn_x(j):
             words = x_raw[j].bitcast(F32)
-            bank = psum.tile([P, 2 * PASSES, P], F32, tag="bank", name="x_bank")
+            bank = psum.tile([P, 2 * PASSES, P], F32, tag="bank", bufs=BANKS - MERGED, name="x_bank")
             for g in range(PASSES):
                 for u in range(2):
                     nc.tensor.transpose(bank[:, 2 * g + u, :], words[:, 256 * g + u : 256 * (g + 1) : 2], ident[:])
             grouped = keep.tile([P, PASSES, P, 2], F32, name="x_grouped%d" % j, align_bytes=64)
             nc.scalar.copy(out=grouped[:], in_=bank[:].rearrange("p (g u) r -> p g r u", u=2))
+            x_grouped[j] = grouped
+
+        def quantize_x(j):
+            grouped = x_grouped[j]
             codes = keep.tile([P, PASSES * P], U32, name="x_codes%d" % j, align_bytes=64)
             scales = keep.tile([P, PASSES * P], U8, name="x_scales%d" % j, align_bytes=64)
             nc.vector.quantize_mx(
@@ -120,18 +146,21 @@ def tile_enhancedmathematicalreasoning_pa_kernel(tc, hidden_states, op_logits, W
             x_codes[j] = codes
             x_scales[j] = scales
 
-        def g_cols(unit, g):
-            return G_COLS if (g == PASSES - 1 and unit >= G_FROM) else 0
-
         def v_cols(unit, g):
             if unit < HEAD_UNITS:
-                return min(HEAD_V, N - g_cols(unit, g))
-            if unit >= UNITS - TAIL_UNITS or g > 0:
-                return 0
-            return BODY_V
+                return (HEAD_V if unit == 0 else HEAD_V1) // 2
+            step = unit
+            n_s = len([j for j in range(TILES) if on_scalar(step - 1, j)]) + (step in BIAS_STEPS)
+            n_v = len([j for j in range(TILES) if not on_scalar(step - 2, j)])
+            if closes(step):
+                n_s += MERGED
+                n_v += MERGED
+            total_cols = BODY_V + STEP_V * (n_s - n_v)
+            if unit >= UNITS - TAIL_UNITS:
+                total_cols = TAIL_V
+            return max(0, min(N, total_cols - N * g))
 
         staged = {}
-        staged_g = {}
 
         def stage_tile(unit, g):
             if (unit, g) not in staged:
@@ -148,18 +177,10 @@ def tile_enhancedmathematicalreasoning_pa_kernel(tc, hidden_states, op_logits, W
                 nc.vector.tensor_copy(out=dst, in_=src)
 
         def copy_s(unit, g):
-            n0, n1 = v_cols(unit, g), N - g_cols(unit, g)
+            n0, n1 = v_cols(unit, g), N
             if n1 > n0:
                 dst, src = views(stage_tile(unit, g)[:, n0:n1, :], w_raw[(unit, g)][:, :, n0:n1])
                 nc.scalar.copy(out=dst, in_=src)
-
-        def copy_g(unit):
-            n = g_cols(unit, PASSES - 1)
-            if n:
-                tile_g = keep.tile([P, n, PACK], BF16, tag="stage_g", name="stage_g", align_bytes=64)
-                staged_g[unit] = tile_g
-                dst, src = views(tile_g[:], w_raw[(unit, PASSES - 1)][:, :, N - n : N])
-                nc.gpsimd.tensor_copy(out=dst, in_=src)
 
         w_codes = {}
         w_scales = {}
@@ -168,103 +189,187 @@ def tile_enhancedmathematicalreasoning_pa_kernel(tc, hidden_states, op_logits, W
             if g == 0:
                 w_codes[unit] = stream.tile([P, PASSES, N], U32, tag="w_codes", name="w_codes", align_bytes=64)
                 w_scales[unit] = stream.tile([P, PASSES, N], U8, tag="w_scales", name="w_scales", align_bytes=64)
-            n1 = N - g_cols(unit, g)
             nc.vector.quantize_mx(
-                out=w_codes[unit][:, g, 0:n1].bitcast(E4M3X4),
-                scales=w_scales[unit][:, g, 0:n1],
-                in_=staged[(unit, g)][:, 0:n1, :].rearrange("p n t -> p (n t)"),
+                out=w_codes[unit][:, g, :].bitcast(E4M3X4),
+                scales=w_scales[unit][:, g, :],
+                in_=staged[(unit, g)][:, :, :].rearrange("p n t -> p (n t)"),
             )
-            if n1 < N:
-                nc.vector.quantize_mx(
-                    out=w_codes[unit][:, g, n1:N].bitcast(E4M3X4),
-                    scales=w_scales[unit][:, g, n1:N],
-                    in_=staged_g[unit][:].rearrange("p n t -> p (n t)"),
-                )
 
         acc = {}
         for j in range(TILES):
             for h in range(HALVES):
                 acc[(j, h)] = keep.tile([P, N], F32, name="acc%d_%d" % (j, h))
 
-        jobs = []
-        drained = [0]
+        banks = {}
+        scaled = {}
+        sums_t = {}
 
-        def drain_oldest():
-            bank, kind, unit, j, h = jobs[drained[0]]
-            drained[0] += 1
-            dst = acc[(j, h)]
-            if kind == "bias":
-                nc.vector.tensor_tensor(out=dst[:], in0=bank[:], in1=dst[:], op=ALU.add)
-                return
-            e = unit // HALVES
-            w_col = gate[:, j * E + e : j * E + e + 1]
-            if e == 0:
-                nc.scalar.activation(out=dst[:], in_=bank[:], func=ACT.Copy, scale=w_col)
-            else:
-                nc.vector.scalar_tensor_tensor(
-                    out=dst[:], in0=bank[:], scalar=w_col, in1=dst[:], op0=ALU.mult, op1=ALU.add
+        def ring_bank():
+            return psum.tile([P, N], F32, tag="bank", bufs=BANKS - MERGED, name="bank")
+
+        def last_merged(h):
+            return LAST_MERGED[h]
+
+        def on_scalar(unit, j):
+            e = unit % E
+            return j < MERGED and e <= last_merged(unit // E)
+
+        def gate_col(unit, j):
+            e = unit % E
+            return gate[:, j * E + e : j * E + e + 1]
+
+        def multiply(unit, j):
+            bank = ring_bank()
+            for g in range(PASSES):
+                nc.tensor.matmul_mx(
+                    out=bank[:],
+                    lhsT=x_codes[j][:, g * P : (g + 1) * P].bitcast(E5M2X4),
+                    lhsT_scale=x_scales[j][:, g * P : (g + 1) * P],
+                    rhs=w_codes[unit][:, g, :].bitcast(E4M3X4),
+                    rhs_scale=w_scales[unit][:, g, :],
+                    start=(g == 0),
+                    stop=(g == PASSES - 1),
                 )
-            if e == E - 1:
-                nc.sync.dma_start(out=out_hbm[:, j, h * N : (h + 1) * N], in_=dst[:])
+            banks[(unit, j)] = bank
 
-        def take_bank():
-            if len(jobs) - drained[0] == BANKS:
-                drain_oldest()
-            return psum.tile([P, N], F32, tag="bank", name="bank")
+        def drain_scalar(unit, j):
+            h, e = divmod(unit, E)
+            if e == 0:
+                dst = acc[(j, h)]
+            else:
+                dst = stream.tile([P, N], F32, tag="scaled", name="scaled", bufs=4)
+                scaled[(unit, j)] = dst
+            nc.scalar.activation(out=dst[:], in_=banks[(unit, j)][:], func=ACT.Copy, scale=gate_col(unit, j))
 
-        def multiply(unit):
-            for j in range(TILES):
-                bank = take_bank()
-                for g in range(PASSES):
-                    nc.tensor.matmul_mx(
-                        out=bank[:],
-                        lhsT=x_codes[j][:, g * P : (g + 1) * P].bitcast(E5M2X4),
-                        lhsT_scale=x_scales[j][:, g * P : (g + 1) * P],
-                        rhs=w_codes[unit][:, g, :].bitcast(E4M3X4),
-                        rhs_scale=w_scales[unit][:, g, :],
-                        start=(g == 0),
-                        stop=(g == PASSES - 1),
-                    )
-                jobs.append((bank, "mx", unit, j, unit % HALVES))
+        def drain_vector(unit, j):
+            h, e = divmod(unit, E)
+            dst = acc[(j, h)]
+            nc.vector.scalar_tensor_tensor(
+                out=dst[:], in0=banks[(unit, j)][:], scalar=gate_col(unit, j), in1=dst[:], op0=ALU.mult, op1=ALU.add
+            )
+
+        def add_bank(bank, j, h):
+            nc.vector.tensor_tensor(out=acc[(j, h)][:], in0=bank[:], in1=acc[(j, h)][:], op=ALU.add)
+
+        def store(j, h):
+            nc.sync.dma_start(out=out_hbm[:, j, h * N : (h + 1) * N], in_=acc[(j, h)][:])
 
         def bias_product(j, h):
-            bank = take_bank()
-            nc.tensor.matmul(bank[:], lhsT=gate_t[:, j, :], rhs=bias32[:, h * N : (h + 1) * N], start=True, stop=True)
-            jobs.append((bank, "bias", 0, j, h))
+            bank = ring_bank()
+            nc.tensor.matmul(bank[:], lhsT=gate_t[:, j, :], rhs=bias_rows[:, h * N : (h + 1) * N], start=True, stop=True)
+            return bank
 
-        quantize_x(0)
-        quantize_x(1)
-        gate_bank = psum.tile([P, TILES, P], F32, tag="bank", name="gate_bank")
-        for j in range(TILES):
-            nc.tensor.transpose(gate_bank[:, j, :], gate[:, j * E : j * E + P], ident[:])
-        quantize_x(2)
+        def start_with_bias(j, h):
+            nc.scalar.copy(out=acc[(j, h)][:], in_=bias_product(j, h)[:])
+
+        def closes(step):
+            past = step - 2
+            return past >= 0 and past % E == last_merged(past // E)
+
+        def open_sum(j, h):
+            sums_t[j] = psum.tile([P, N // P, P], F32, tag="sum_t%d" % j, name="sum_t")
+            for b in range(N // P):
+                cols = slice(h * N + b * P, h * N + (b + 1) * P)
+                nc.tensor.matmul(sums_t[j][:, b, :], lhsT=bias_rows[:, cols], rhs=gate_t[:, j, :], start=(b == 0), stop=False)
+
+        def add_transposed(unit, j):
+            last = unit % E == last_merged(unit // E)
+            for b in range(N // P):
+                nc.tensor.matmul(
+                    sums_t[j][:, b, :],
+                    lhsT=scaled[(unit, j)][:, b * P : (b + 1) * P],
+                    rhs=ident[:],
+                    is_transpose=True,
+                    start=False,
+                    stop=(last and b == N // P - 1),
+                )
+
+        def close_sum(j):
+            turned = stream.tile([P, N // P, P], F32, tag="scaled", name="turned", bufs=4)
+            nc.scalar.copy(out=turned[:], in_=sums_t[j][:])
+            return turned
+
+        def turn_back(turned):
+            bank = ring_bank()
+            for b in range(N // P):
+                nc.tensor.transpose(bank[:, b * P : (b + 1) * P], turned[:, b, :], ident[:])
+            return bank
+
+        turn_x(0)
         copy_v(0, 0)
-        quantize_x(3)
-        gate_t = keep.tile([P, TILES, P], F32)
-        nc.scalar.copy(out=gate_t[:], in_=gate_bank[:])
         copy_s(0, 0)
+        nc.vector.tensor_copy(out=part_view[:, :, 0, :], in_=gate_view)
+        quantize_x(0)
+        turn_x(1)
+        nc.vector.tensor_tensor(out=rest[:], in0=gate_view, in1=part_view[:, :, 0, :], op=ALU.subtract)
+        quantize_w(0, 0)
+        nc.vector.tensor_copy(out=part_view[:, :, 1, :], in_=rest[:])
+        quantize_x(1)
+        nc.vector.tensor_tensor(out=part_view[:, :, 2, :], in0=rest[:], in1=part_view[:, :, 1, :], op=ALU.subtract)
         copy_v(0, 1)
         copy_s(0, 1)
-        quantize_w(0, 0)
+        turn_x(2)
+        gate_bank = psum.tile([P, TILES, P], BF16, tag="bank", bufs=BANKS - MERGED, name="gate_bank")
+        for j in range(TILES):
+            nc.tensor.transpose(gate_bank[:, j, :], parts[:, j * PARTS * E : j * PARTS * E + P], ident16[:])
+        turn_x(3)
+        gate_t = keep.tile([P, TILES, P], BF16)
+        nc.scalar.copy(out=gate_t[:], in_=gate_bank[:])
+        if LEAD_S:
+            copy_s(1, 0)
+            copy_s(1, 1)
 
         for step in range(1, UNITS + 2):
+            now = step - 1
+            past = step - 2
+            closing = closes(step)
+            if now < UNITS:
+                if now > 0:
+                    quantize_w(now, 0)
+                quantize_w(now, 1)
+            if step == 1:
+                quantize_x(2)
+                quantize_x(3)
+            finished = []
+            if closing:
+                for m in range(MERGED):
+                    finished.append((turn_back(close_sum(m)), m, past // E))
             if step < UNITS:
                 copy_v(step, 0)
-            if step <= UNITS:
-                if step > 1:
-                    quantize_w(step - 1, 0)
-                quantize_w(step - 1, 1)
-            if step < UNITS:
-                copy_g(step)
-                copy_s(step, 0)
                 copy_v(step, 1)
-            older = len(jobs)
-            if step <= UNITS:
-                multiply(step - 1)
-            i = step - BIAS_FROM
-            if 0 <= i < TILES * HALVES:
-                bias_product(i // HALVES, step % HALVES)
-            for job in range(drained[0], older):
-                drain_oldest()
-            if step < UNITS:
-                copy_s(step, 1)
+            if step + LEAD_S < UNITS:
+                copy_s(step + LEAD_S, 0)
+                copy_s(step + LEAD_S, 1)
+            if step in BIAS_STEPS:
+                start_with_bias(MERGED + BIAS_STEPS.index(step), 1)
+            if step == HEAD_BIAS:
+                for j in range(MERGED, TILES):
+                    start_with_bias(j, 0)
+            held = len(finished)
+            if past >= 0:
+                held += len([j for j in range(TILES) if not on_scalar(past, j)])
+            early = min(TILES, BANKS - MERGED - held) if now < UNITS else 0
+            for j in range(early):
+                multiply(now, j)
+            if past >= 0:
+                for j in range(TILES):
+                    if not on_scalar(past, j):
+                        drain_vector(past, j)
+                        if past % E == E - 1:
+                            store(j, past // E)
+            for bank, j, h in finished:
+                add_bank(bank, j, h)
+                if last_merged(h) == E - 1:
+                    store(j, h)
+            if now < UNITS:
+                for j in range(early, TILES):
+                    multiply(now, j)
+                for j in range(TILES):
+                    if on_scalar(now, j):
+                        drain_scalar(now, j)
+                if now % E == 0:
+                    for m in range(MERGED):
+                        open_sum(m, now // E)
+                elif now % E <= last_merged(now // E):
+                    for m in range(MERGED):
+                        add_transposed(now, m)

@@ -22,25 +22,24 @@ K_PASS = P * PACK
 PASSES = H // K_PASS
 TILES = TOKENS // P
 N = 512
+BLOCKS = N // P
 HALVES = HO // N
-UNITS = E * HALVES
-BANKS = 8
-
-MERGED = 2
-LAST_MERGED = (7, 6)
-HEAD_UNITS = 2
-HEAD_V = 512
-BODY_V = 512
-STEP_V = 64
-HEAD_BIAS = 1
-HEAD_V1 = 896
-TAIL_V = 512
-TAIL_UNITS = 1
-LEAD_S = 0
-BIAS_STEPS = (4, 6)
-W_FIRST = 0
-RUN = 4
+UNITS = HALVES * E
 PARTS = 3
+
+SCALAR_TILES = (0, 1)
+VECTOR_TILES = (2, 3)
+RING_BANKS = 8 - len(SCALAR_TILES)
+STAGE_BUFS = 6
+CODE_BUFS = 3
+SCALED_BUFS = 4
+
+HEAD_VECTOR_COLS = 384
+VECTOR_COLS = 512
+COLS_PER_BANK = 96
+HEAD_UNITS = 2
+RUN = 4
+LATE_BIAS_STEPS = (3, 5)
 
 
 def tile_enhancedmathematicalreasoning_pa_kernel(tc, hidden_states, op_logits, We, be, out):
@@ -51,49 +50,44 @@ def tile_enhancedmathematicalreasoning_pa_kernel(tc, hidden_states, op_logits, W
 
     with ExitStack() as ctx:
         keep = ctx.enter_context(tc.tile_pool(name="keep", bufs=1))
-        stream = ctx.enter_context(tc.tile_pool(name="stream", bufs=3))
+        stream = ctx.enter_context(tc.tile_pool(name="stream", bufs=CODE_BUFS))
         psum = ctx.enter_context(tc.psum_pool(name="psum", bufs=1))
         ctx.enter_context(tc.manual_schedule())
 
         logits = keep.tile([P, TILES, E], BF16)
-        nc.sync.dma_start(out=logits[:], in_=logits_hbm)
+        nc.scalar.dma_start(out=logits[:], in_=logits_hbm)
         bias_rows = keep.tile([P, HO], BF16)
         nc.vector.memset(bias_rows[:], 0.0)
         for part in range(PARTS):
             nc.scalar.dma_start(out=bias_rows[part * E : (part + 1) * E, :], in_=be)
+
         x_raw = {}
         w_raw = {}
 
         def load_x(j):
-            x_tile = keep.tile([P, H], BF16, name="x_tile%d" % j)
-            nc.sync.dma_start(out=x_tile[:], in_=x_hbm[:, j, :])
-            x_raw[j] = x_tile[:]
+            x_raw[j] = keep.tile([P, H], BF16, name="x_raw%d" % j)
+            nc.sync.dma_start(out=x_raw[j][:], in_=x_hbm[:, j, :])
 
         def load_w(unit, g):
             h, e = divmod(unit, E)
-            piece = keep.tile([P, PACK, N], BF16, name="w%d_%d" % (unit, g))
+            w_raw[(unit, g)] = keep.tile([P, PACK, N], BF16, name="w_raw%d_%d" % (unit, g))
             rows = We[e, g * K_PASS : (g + 1) * K_PASS, h * N : (h + 1) * N]
-            nc.sync.dma_start(out=piece[:], in_=rows.rearrange("(p t) n -> p t n", t=PACK))
-            w_raw[(unit, g)] = piece[:]
+            nc.sync.dma_start(out=w_raw[(unit, g)][:], in_=rows.rearrange("(p t) n -> p t n", t=PACK))
 
-        if W_FIRST == 0:
-            load_x(0)
+        load_x(0)
         load_w(0, 0)
-        if W_FIRST == 1:
-            load_x(0)
         load_x(1)
-        load_w(0, 1)
         load_x(2)
+        load_w(0, 1)
         load_x(3)
         for unit in range(1, UNITS):
             for g in range(PASSES):
                 load_w(unit, g)
 
-        ident = keep.tile([P, P], F32)
-        make_identity(nc, ident[:])
+        ident32 = keep.tile([P, P], F32)
+        make_identity(nc, ident32[:])
         ident16 = keep.tile([P, P], BF16)
         make_identity(nc, ident16[:])
-        gate = keep.tile([P, TILES * E], F32)
         parts = keep.tile([P, (TILES - 1) * PARTS * E + P], BF16)
         nc.gpsimd.memset(parts[:], 0.0)
 
@@ -103,87 +97,81 @@ def tile_enhancedmathematicalreasoning_pa_kernel(tc, hidden_states, op_logits, W
         nc.vector.tensor_tensor(
             out=shifted[:], in0=logits[:], in1=top[:].unsqueeze(2).to_broadcast([P, TILES, E]), op=ALU.subtract
         )
-        ex = keep.tile([P, TILES, E], F32)
-        nc.scalar.activation(out=ex[:], in_=shifted[:], func=ACT.Exp)
+        exps = keep.tile([P, TILES, E], F32)
+        nc.scalar.activation(out=exps[:], in_=shifted[:], func=ACT.Exp)
         total = keep.tile([P, TILES], F32)
-        nc.vector.tensor_reduce(out=total[:], in_=ex[:], axis=AX.X, op=ALU.add)
-        inv = keep.tile([P, TILES], F32)
-        nc.vector.reciprocal(out=inv[:], in_=total[:])
+        nc.vector.tensor_reduce(out=total[:], in_=exps[:], axis=AX.X, op=ALU.add)
+        inverse = keep.tile([P, TILES], F32)
+        nc.vector.reciprocal(out=inverse[:], in_=total[:])
+        gate = keep.tile([P, TILES, E], F32)
         nc.vector.tensor_tensor(
-            out=gate[:, 0 : TILES * E].rearrange("p (j e) -> p j e", e=E),
-            in0=ex[:],
-            in1=inv[:].unsqueeze(2).to_broadcast([P, TILES, E]),
-            op=ALU.mult,
+            out=gate[:], in0=exps[:], in1=inverse[:].unsqueeze(2).to_broadcast([P, TILES, E]), op=ALU.mult
         )
-        part_view = parts[:, 0 : TILES * PARTS * E].rearrange("p (j q e) -> p j q e", q=PARTS, e=E)
-        gate_view = gate[:].rearrange("p (j e) -> p j e", e=E)
-        rest = keep.tile([P, TILES, E], F32)
 
+        def ring_bank(shape, dtype):
+            return psum.tile(shape, dtype, tag="ring", bufs=RING_BANKS, name="ring")
+
+        x_grouped = {}
         x_codes = {}
         x_scales = {}
 
-        x_grouped = {}
-
         def turn_x(j):
-            words = x_raw[j].bitcast(F32)
-            bank = psum.tile([P, 2 * PASSES, P], F32, tag="bank", bufs=BANKS - MERGED, name="x_bank")
+            words = x_raw[j][:].bitcast(F32)
+            pass_words = K_PASS // 2
+            bank = ring_bank([P, PASSES * 2, P], F32)
             for g in range(PASSES):
                 for u in range(2):
-                    nc.tensor.transpose(bank[:, 2 * g + u, :], words[:, 256 * g + u : 256 * (g + 1) : 2], ident[:])
-            grouped = keep.tile([P, PASSES, P, 2], F32, name="x_grouped%d" % j, align_bytes=64)
-            nc.scalar.copy(out=grouped[:], in_=bank[:].rearrange("p (g u) r -> p g r u", u=2))
-            x_grouped[j] = grouped
+                    picked = words[:, g * pass_words + u : (g + 1) * pass_words : 2]
+                    nc.tensor.transpose(bank[:, 2 * g + u, :], picked, ident32[:])
+            x_grouped[j] = keep.tile([P, PASSES, P, 2], F32, name="x_grouped%d" % j, align_bytes=64)
+            nc.scalar.copy(out=x_grouped[j][:], in_=bank[:].rearrange("p (g u) r -> p g r u", u=2))
 
         def quantize_x(j):
-            grouped = x_grouped[j]
-            codes = keep.tile([P, PASSES * P], U32, name="x_codes%d" % j, align_bytes=64)
-            scales = keep.tile([P, PASSES * P], U8, name="x_scales%d" % j, align_bytes=64)
+            x_codes[j] = keep.tile([P, PASSES * P], U32, name="x_codes%d" % j, align_bytes=64)
+            x_scales[j] = keep.tile([P, PASSES * P], U8, name="x_scales%d" % j, align_bytes=64)
             nc.vector.quantize_mx(
-                out=codes[:].bitcast(E5M2X4),
-                scales=scales[:],
-                in_=grouped[:].rearrange("p g r u -> p (g r u)").bitcast(BF16),
+                out=x_codes[j][:].bitcast(E5M2X4),
+                scales=x_scales[j][:],
+                in_=x_grouped[j][:].rearrange("p g r u -> p (g r u)").bitcast(BF16),
             )
-            x_codes[j] = codes
-            x_scales[j] = scales
 
-        def v_cols(unit, g):
-            if unit < HEAD_UNITS:
-                return (HEAD_V if unit == 0 else HEAD_V1) // 2
-            step = unit
-            n_s = len([j for j in range(TILES) if on_scalar(step - 1, j)]) + (step in BIAS_STEPS)
-            n_v = len([j for j in range(TILES) if not on_scalar(step - 2, j)])
-            if closes(step):
-                n_s += MERGED
-                n_v += MERGED
-            total_cols = BODY_V + STEP_V * (n_s - n_v)
-            if unit >= UNITS - TAIL_UNITS:
-                total_cols = TAIL_V
-            return max(0, min(N, total_cols - N * g))
+        def scalar_tiles(unit):
+            return SCALAR_TILES if unit % E < E - 1 else ()
+
+        def vector_tiles(unit):
+            return VECTOR_TILES if unit % E < E - 1 else VECTOR_TILES + SCALAR_TILES
+
+        def closing_tiles(step):
+            return SCALAR_TILES if (step - 2) % E == E - 2 else ()
 
         staged = {}
-
-        def stage_tile(unit, g):
-            if (unit, g) not in staged:
-                staged[(unit, g)] = stream.tile([P, N, PACK], BF16, tag="stage", name="stage", bufs=6, align_bytes=64)
-            return staged[(unit, g)]
-
-        def views(dst, src):
-            return dst.rearrange("p (c i) t -> p c t i", i=RUN), src.rearrange("p t (c i) -> p c t i", i=RUN)
-
-        def copy_v(unit, g):
-            n = v_cols(unit, g)
-            if n:
-                dst, src = views(stage_tile(unit, g)[:, 0:n, :], w_raw[(unit, g)][:, :, 0:n])
-                nc.vector.tensor_copy(out=dst, in_=src)
-
-        def copy_s(unit, g):
-            n0, n1 = v_cols(unit, g), N
-            if n1 > n0:
-                dst, src = views(stage_tile(unit, g)[:, n0:n1, :], w_raw[(unit, g)][:, :, n0:n1])
-                nc.scalar.copy(out=dst, in_=src)
-
         w_codes = {}
         w_scales = {}
+
+        def vector_cols(unit, g):
+            if unit < HEAD_UNITS:
+                return HEAD_VECTOR_COLS
+            scalar_banks = len(scalar_tiles(unit - 1)) + 2 * len(closing_tiles(unit)) + (unit in LATE_BIAS_STEPS)
+            cols = VECTOR_COLS + COLS_PER_BANK * (scalar_banks - len(vector_tiles(unit - 2)))
+            return max(0, min(N, cols - g * N))
+
+        def interleave(copy, unit, g, first, last):
+            if first == last:
+                return
+            if (unit, g) not in staged:
+                staged[(unit, g)] = stream.tile(
+                    [P, N, PACK], BF16, tag="staged", name="staged", bufs=STAGE_BUFS, align_bytes=64
+                )
+            copy(
+                out=staged[(unit, g)][:, first:last, :].rearrange("p (c i) t -> p c t i", i=RUN),
+                in_=w_raw[(unit, g)][:, :, first:last].rearrange("p t (c i) -> p c t i", i=RUN),
+            )
+
+        def interleave_on_vector(unit, g):
+            interleave(nc.vector.tensor_copy, unit, g, 0, vector_cols(unit, g))
+
+        def interleave_on_scalar(unit, g):
+            interleave(nc.scalar.copy, unit, g, vector_cols(unit, g), N)
 
         def quantize_w(unit, g):
             if g == 0:
@@ -192,37 +180,23 @@ def tile_enhancedmathematicalreasoning_pa_kernel(tc, hidden_states, op_logits, W
             nc.vector.quantize_mx(
                 out=w_codes[unit][:, g, :].bitcast(E4M3X4),
                 scales=w_scales[unit][:, g, :],
-                in_=staged[(unit, g)][:, :, :].rearrange("p n t -> p (n t)"),
+                in_=staged[(unit, g)][:].rearrange("p n t -> p (n t)"),
             )
 
         acc = {}
         for j in range(TILES):
             for h in range(HALVES):
                 acc[(j, h)] = keep.tile([P, N], F32, name="acc%d_%d" % (j, h))
-
-        banks = {}
+        gate_t = keep.tile([P, TILES, P], BF16)
+        product = {}
         scaled = {}
-        sums_t = {}
-
-        def ring_bank():
-            return psum.tile([P, N], F32, tag="bank", bufs=BANKS - MERGED, name="bank")
-
-        def last_merged(h):
-            return LAST_MERGED[h]
-
-        def on_scalar(unit, j):
-            e = unit % E
-            return j < MERGED and e <= last_merged(unit // E)
-
-        def gate_col(unit, j):
-            e = unit % E
-            return gate[:, j * E + e : j * E + e + 1]
+        sum_t = {}
 
         def multiply(unit, j):
-            bank = ring_bank()
+            product[(unit, j)] = ring_bank([P, N], F32)
             for g in range(PASSES):
                 nc.tensor.matmul_mx(
-                    out=bank[:],
+                    out=product[(unit, j)][:],
                     lhsT=x_codes[j][:, g * P : (g + 1) * P].bitcast(E5M2X4),
                     lhsT_scale=x_scales[j][:, g * P : (g + 1) * P],
                     rhs=w_codes[unit][:, g, :].bitcast(E4M3X4),
@@ -230,146 +204,143 @@ def tile_enhancedmathematicalreasoning_pa_kernel(tc, hidden_states, op_logits, W
                     start=(g == 0),
                     stop=(g == PASSES - 1),
                 )
-            banks[(unit, j)] = bank
 
-        def drain_scalar(unit, j):
-            h, e = divmod(unit, E)
-            if e == 0:
-                dst = acc[(j, h)]
-            else:
-                dst = stream.tile([P, N], F32, tag="scaled", name="scaled", bufs=4)
-                scaled[(unit, j)] = dst
-            nc.scalar.activation(out=dst[:], in_=banks[(unit, j)][:], func=ACT.Copy, scale=gate_col(unit, j))
+        def gate_column(unit, j):
+            return gate[:, j, unit % E : unit % E + 1]
 
-        def drain_vector(unit, j):
-            h, e = divmod(unit, E)
-            dst = acc[(j, h)]
+        def scaled_tile():
+            return stream.tile([P, N], F32, tag="scaled", name="scaled", bufs=SCALED_BUFS)
+
+        def add_on_vector(unit, j):
+            h = unit // E
             nc.vector.scalar_tensor_tensor(
-                out=dst[:], in0=banks[(unit, j)][:], scalar=gate_col(unit, j), in1=dst[:], op0=ALU.mult, op1=ALU.add
+                out=acc[(j, h)][:],
+                in0=product[(unit, j)][:],
+                scalar=gate_column(unit, j),
+                in1=acc[(j, h)][:],
+                op0=ALU.mult,
+                op1=ALU.add,
+            )
+            if unit % E == E - 1:
+                nc.sync.dma_start(out=out_hbm[:, j, h * N : (h + 1) * N], in_=acc[(j, h)][:])
+
+        def scale_on_scalar(unit, j):
+            scaled[(unit, j)] = scaled_tile()
+            nc.scalar.activation(
+                out=scaled[(unit, j)][:], in_=product[(unit, j)][:], func=ACT.Copy, scale=gate_column(unit, j)
             )
 
-        def add_bank(bank, j, h):
-            nc.vector.tensor_tensor(out=acc[(j, h)][:], in0=bank[:], in1=acc[(j, h)][:], op=ALU.add)
-
-        def store(j, h):
-            nc.sync.dma_start(out=out_hbm[:, j, h * N : (h + 1) * N], in_=acc[(j, h)][:])
-
-        def bias_product(j, h):
-            bank = ring_bank()
+        def bias_term(j, h):
+            bank = ring_bank([P, N], F32)
             nc.tensor.matmul(bank[:], lhsT=gate_t[:, j, :], rhs=bias_rows[:, h * N : (h + 1) * N], start=True, stop=True)
             return bank
 
-        def start_with_bias(j, h):
-            nc.scalar.copy(out=acc[(j, h)][:], in_=bias_product(j, h)[:])
-
-        def closes(step):
-            past = step - 2
-            return past >= 0 and past % E == last_merged(past // E)
-
         def open_sum(j, h):
-            sums_t[j] = psum.tile([P, N // P, P], F32, tag="sum_t%d" % j, name="sum_t")
-            for b in range(N // P):
+            sum_t[j] = psum.tile([P, BLOCKS, P], F32, tag="sum_t%d" % j, name="sum_t")
+            for b in range(BLOCKS):
                 cols = slice(h * N + b * P, h * N + (b + 1) * P)
-                nc.tensor.matmul(sums_t[j][:, b, :], lhsT=bias_rows[:, cols], rhs=gate_t[:, j, :], start=(b == 0), stop=False)
-
-        def add_transposed(unit, j):
-            last = unit % E == last_merged(unit // E)
-            for b in range(N // P):
                 nc.tensor.matmul(
-                    sums_t[j][:, b, :],
-                    lhsT=scaled[(unit, j)][:, b * P : (b + 1) * P],
-                    rhs=ident[:],
-                    is_transpose=True,
-                    start=False,
-                    stop=(last and b == N // P - 1),
+                    sum_t[j][:, b, :], lhsT=bias_rows[:, cols], rhs=gate_t[:, j, :], start=(b == 0), stop=False
                 )
 
-        def close_sum(j):
-            turned = stream.tile([P, N // P, P], F32, tag="scaled", name="turned", bufs=4)
-            nc.scalar.copy(out=turned[:], in_=sums_t[j][:])
+        def add_transposed(unit, j):
+            for b in range(BLOCKS):
+                nc.tensor.matmul(
+                    sum_t[j][:, b, :],
+                    lhsT=scaled[(unit, j)][:, b * P : (b + 1) * P],
+                    rhs=ident32[:],
+                    is_transpose=True,
+                    start=False,
+                    stop=(unit % E == E - 2 and b == BLOCKS - 1),
+                )
+
+        def read_sum(j):
+            turned = scaled_tile()
+            nc.scalar.copy(out=turned[:], in_=sum_t[j][:].rearrange("p b r -> p (b r)"))
             return turned
 
-        def turn_back(turned):
-            bank = ring_bank()
-            for b in range(N // P):
-                nc.tensor.transpose(bank[:, b * P : (b + 1) * P], turned[:, b, :], ident[:])
-            return bank
+        def turn_back(turned, j, h):
+            bank = ring_bank([P, N], F32)
+            for b in range(BLOCKS):
+                cols = slice(b * P, (b + 1) * P)
+                nc.tensor.transpose(bank[:, cols], turned[:, cols], ident32[:])
+            nc.scalar.copy(out=acc[(j, h)][:], in_=bank[:])
 
+        part_view = parts[:, 0 : TILES * PARTS * E].rearrange("p (j q e) -> p j q e", q=PARTS, e=E)
+        rest = keep.tile([P, TILES, E], F32)
+        nc.vector.tensor_copy(out=part_view[:, :, 0, :], in_=gate[:])
         turn_x(0)
-        copy_v(0, 0)
-        copy_s(0, 0)
-        nc.vector.tensor_copy(out=part_view[:, :, 0, :], in_=gate_view)
+        interleave_on_vector(0, 0)
+        interleave_on_scalar(0, 0)
+        nc.vector.tensor_tensor(out=rest[:], in0=gate[:], in1=part_view[:, :, 0, :], op=ALU.subtract)
         quantize_x(0)
-        turn_x(1)
-        nc.vector.tensor_tensor(out=rest[:], in0=gate_view, in1=part_view[:, :, 0, :], op=ALU.subtract)
-        quantize_w(0, 0)
         nc.vector.tensor_copy(out=part_view[:, :, 1, :], in_=rest[:])
-        quantize_x(1)
+        turn_x(1)
         nc.vector.tensor_tensor(out=part_view[:, :, 2, :], in0=rest[:], in1=part_view[:, :, 1, :], op=ALU.subtract)
-        copy_v(0, 1)
-        copy_s(0, 1)
-        turn_x(2)
-        gate_bank = psum.tile([P, TILES, P], BF16, tag="bank", bufs=BANKS - MERGED, name="gate_bank")
+        quantize_w(0, 0)
+        gate_bank = ring_bank([P, TILES, P], BF16)
         for j in range(TILES):
-            nc.tensor.transpose(gate_bank[:, j, :], parts[:, j * PARTS * E : j * PARTS * E + P], ident16[:])
-        turn_x(3)
-        gate_t = keep.tile([P, TILES, P], BF16)
+            first = j * PARTS * E
+            nc.tensor.transpose(gate_bank[:, j, :], parts[:, first : first + P], ident16[:])
+        quantize_x(1)
+        interleave_on_vector(0, 1)
         nc.scalar.copy(out=gate_t[:], in_=gate_bank[:])
-        if LEAD_S:
-            copy_s(1, 0)
-            copy_s(1, 1)
+        turn_x(2)
+        interleave_on_scalar(0, 1)
+        turn_x(3)
+        first_bias = [bias_term(j, 0) for j in VECTOR_TILES]
+        quantize_x(2)
+        quantize_w(0, 1)
+        for j in SCALAR_TILES:
+            open_sum(j, 0)
+        for j in range(TILES - 1):
+            multiply(0, j)
+        quantize_x(3)
+        for j, bank in zip(VECTOR_TILES, first_bias):
+            nc.scalar.copy(out=acc[(j, 0)][:], in_=bank[:])
+        multiply(0, TILES - 1)
+        for g in range(PASSES):
+            interleave_on_vector(1, g)
+        for g in range(PASSES):
+            interleave_on_scalar(1, g)
+        for j in SCALAR_TILES:
+            scale_on_scalar(0, j)
+        for j in SCALAR_TILES:
+            add_transposed(0, j)
 
-        for step in range(1, UNITS + 2):
+        for step in range(2, UNITS + 1):
             now = step - 1
             past = step - 2
-            closing = closes(step)
-            if now < UNITS:
-                if now > 0:
-                    quantize_w(now, 0)
-                quantize_w(now, 1)
-            if step == 1:
-                quantize_x(2)
-                quantize_x(3)
-            finished = []
-            if closing:
-                for m in range(MERGED):
-                    finished.append((turn_back(close_sum(m)), m, past // E))
+            for g in range(PASSES):
+                quantize_w(now, g)
+            turned = [read_sum(j) for j in closing_tiles(step)]
             if step < UNITS:
-                copy_v(step, 0)
-                copy_v(step, 1)
-            if step + LEAD_S < UNITS:
-                copy_s(step + LEAD_S, 0)
-                copy_s(step + LEAD_S, 1)
-            if step in BIAS_STEPS:
-                start_with_bias(MERGED + BIAS_STEPS.index(step), 1)
-            if step == HEAD_BIAS:
-                for j in range(MERGED, TILES):
-                    start_with_bias(j, 0)
-            held = len(finished)
-            if past >= 0:
-                held += len([j for j in range(TILES) if not on_scalar(past, j)])
-            early = min(TILES, BANKS - MERGED - held) if now < UNITS else 0
-            for j in range(early):
+                for g in range(PASSES):
+                    interleave_on_vector(step, g)
+                for g in range(PASSES):
+                    interleave_on_scalar(step, g)
+            if step in LATE_BIAS_STEPS:
+                j = VECTOR_TILES[LATE_BIAS_STEPS.index(step)]
+                nc.scalar.copy(out=acc[(j, 1)][:], in_=bias_term(j, 1)[:])
+            if now % E == 0:
+                for j in SCALAR_TILES:
+                    open_sum(j, now // E)
+
+            order = scalar_tiles(now) + vector_tiles(now)
+            free = min(TILES, RING_BANKS - len(turned) - len(vector_tiles(past)))
+            multiply(now, order[0])
+            for j, tile_t in zip(closing_tiles(step), turned):
+                turn_back(tile_t, j, past // E)
+            for j in order[1:free]:
                 multiply(now, j)
-            if past >= 0:
-                for j in range(TILES):
-                    if not on_scalar(past, j):
-                        drain_vector(past, j)
-                        if past % E == E - 1:
-                            store(j, past // E)
-            for bank, j, h in finished:
-                add_bank(bank, j, h)
-                if last_merged(h) == E - 1:
-                    store(j, h)
-            if now < UNITS:
-                for j in range(early, TILES):
-                    multiply(now, j)
-                for j in range(TILES):
-                    if on_scalar(now, j):
-                        drain_scalar(now, j)
-                if now % E == 0:
-                    for m in range(MERGED):
-                        open_sum(m, now // E)
-                elif now % E <= last_merged(now // E):
-                    for m in range(MERGED):
-                        add_transposed(now, m)
+            for j in vector_tiles(past):
+                add_on_vector(past, j)
+            for j in order[free:]:
+                multiply(now, j)
+            for j in scalar_tiles(now):
+                scale_on_scalar(now, j)
+            for j in scalar_tiles(now):
+                add_transposed(now, j)
+
+        for j in vector_tiles(UNITS - 1):
+            add_on_vector(UNITS - 1, j)

@@ -35,9 +35,11 @@ CODE_BUFS = 3
 SCALED_BUFS = 4
 
 HEAD_VECTOR_COLS = 384
-VECTOR_COLS = 512
-COLS_PER_BANK = 96
+VECTOR_COLS = 416
+COLS_PER_BANK = 64
 HEAD_UNITS = 2
+GPSIMD_COLS = 128
+GPSIMD_FROM = 3
 RUN = 4
 LATE_BIAS_STEPS = (3, 5)
 
@@ -153,7 +155,7 @@ def tile_enhancedmathematicalreasoning_pa_kernel(tc, hidden_states, op_logits, W
                 return HEAD_VECTOR_COLS
             scalar_banks = len(scalar_tiles(unit - 1)) + 2 * len(closing_tiles(unit)) + (unit in LATE_BIAS_STEPS)
             cols = VECTOR_COLS + COLS_PER_BANK * (scalar_banks - len(vector_tiles(unit - 2)))
-            return max(0, min(N, cols - g * N))
+            return max(0, min(N - gpsimd_cols(unit, g), cols - g * N))
 
         def interleave(copy, unit, g, first, last):
             if first == last:
@@ -170,18 +172,39 @@ def tile_enhancedmathematicalreasoning_pa_kernel(tc, hidden_states, op_logits, W
         def interleave_on_vector(unit, g):
             interleave(nc.vector.tensor_copy, unit, g, 0, vector_cols(unit, g))
 
+        def gpsimd_cols(unit, g):
+            return GPSIMD_COLS if g == PASSES - 1 and unit >= GPSIMD_FROM else 0
+
         def interleave_on_scalar(unit, g):
-            interleave(nc.scalar.copy, unit, g, vector_cols(unit, g), N)
+            interleave(nc.scalar.copy, unit, g, vector_cols(unit, g), N - gpsimd_cols(unit, g))
+
+        staged_last = {}
+
+        def interleave_on_gpsimd(unit):
+            staged_last[unit] = keep.tile(
+                [P, GPSIMD_COLS, PACK], BF16, tag="staged_last", name="staged_last", align_bytes=64
+            )
+            nc.gpsimd.tensor_copy(
+                out=staged_last[unit][:],
+                in_=w_raw[(unit, PASSES - 1)][:, :, N - GPSIMD_COLS : N].rearrange("p t n -> p n t"),
+            )
 
         def quantize_w(unit, g):
             if g == 0:
                 w_codes[unit] = stream.tile([P, PASSES, N], U32, tag="w_codes", name="w_codes", align_bytes=64)
                 w_scales[unit] = stream.tile([P, PASSES, N], U8, tag="w_scales", name="w_scales", align_bytes=64)
+            cut = N - gpsimd_cols(unit, g)
             nc.vector.quantize_mx(
-                out=w_codes[unit][:, g, :].bitcast(E4M3X4),
-                scales=w_scales[unit][:, g, :],
-                in_=staged[(unit, g)][:].rearrange("p n t -> p (n t)"),
+                out=w_codes[unit][:, g, 0:cut].bitcast(E4M3X4),
+                scales=w_scales[unit][:, g, 0:cut],
+                in_=staged[(unit, g)][:, 0:cut, :].rearrange("p n t -> p (n t)"),
             )
+            if cut < N:
+                nc.vector.quantize_mx(
+                    out=w_codes[unit][:, g, cut:N].bitcast(E4M3X4),
+                    scales=w_scales[unit][:, g, cut:N],
+                    in_=staged_last[unit][:].rearrange("p n t -> p (n t)"),
+                )
 
         acc = {}
         for j in range(TILES):
@@ -311,12 +334,15 @@ def tile_enhancedmathematicalreasoning_pa_kernel(tc, hidden_states, op_logits, W
         for step in range(2, UNITS + 1):
             now = step - 1
             past = step - 2
+            if step < UNITS:
+                for g in range(PASSES):
+                    interleave_on_vector(step, g)
             for g in range(PASSES):
                 quantize_w(now, g)
             turned = [read_sum(j) for j in closing_tiles(step)]
             if step < UNITS:
-                for g in range(PASSES):
-                    interleave_on_vector(step, g)
+                if step >= GPSIMD_FROM:
+                    interleave_on_gpsimd(step)
                 for g in range(PASSES):
                     interleave_on_scalar(step, g)
             if step in LATE_BIAS_STEPS:

@@ -27,21 +27,20 @@ HALVES = HO // N
 UNITS = HALVES * E
 PARTS = 3
 
-SCALAR_TILES = (0, 1)
-VECTOR_TILES = (2, 3)
+SCALAR_TILES = (0,)
+VECTOR_TILES = (1, 2, 3)
 RING_BANKS = 8 - len(SCALAR_TILES)
 STAGE_BUFS = 6
 CODE_BUFS = 3
-SCALED_BUFS = 4
+SCALED_BUFS = 2
 
-HEAD_VECTOR_COLS = 384
-VECTOR_COLS = 416
+HEAD_VECTOR_COLS = 448
+VECTOR_COLS = 304
 COLS_PER_BANK = 64
 HEAD_UNITS = 2
-GPSIMD_COLS = 128
-GPSIMD_FROM = 3
+GPSIMD_COLS = 256
 RUN = 4
-LATE_BIAS_STEPS = (3, 5)
+LATE_BIAS_STEPS = (3, 4, 5)
 
 
 def tile_enhancedmathematicalreasoning_pa_kernel(tc, hidden_states, op_logits, We, be, out):
@@ -153,13 +152,12 @@ def tile_enhancedmathematicalreasoning_pa_kernel(tc, hidden_states, op_logits, W
         def vector_cols(unit, g):
             if unit < HEAD_UNITS:
                 return HEAD_VECTOR_COLS
+            if g > 0:
+                return 0
             scalar_banks = len(scalar_tiles(unit - 1)) + 2 * len(closing_tiles(unit)) + (unit in LATE_BIAS_STEPS)
-            cols = VECTOR_COLS + COLS_PER_BANK * (scalar_banks - len(vector_tiles(unit - 2)))
-            return max(0, min(N - gpsimd_cols(unit, g), cols - g * N))
+            return VECTOR_COLS + COLS_PER_BANK * (scalar_banks - len(vector_tiles(unit - 2)))
 
         def interleave(copy, unit, g, first, last):
-            if first == last:
-                return
             if (unit, g) not in staged:
                 staged[(unit, g)] = stream.tile(
                     [P, N, PACK], BF16, tag="staged", name="staged", bufs=STAGE_BUFS, align_bytes=64
@@ -173,7 +171,7 @@ def tile_enhancedmathematicalreasoning_pa_kernel(tc, hidden_states, op_logits, W
             interleave(nc.vector.tensor_copy, unit, g, 0, vector_cols(unit, g))
 
         def gpsimd_cols(unit, g):
-            return GPSIMD_COLS if g == PASSES - 1 and unit >= GPSIMD_FROM else 0
+            return GPSIMD_COLS if g == PASSES - 1 and unit >= HEAD_UNITS else 0
 
         def interleave_on_scalar(unit, g):
             interleave(nc.scalar.copy, unit, g, vector_cols(unit, g), N - gpsimd_cols(unit, g))
@@ -194,17 +192,17 @@ def tile_enhancedmathematicalreasoning_pa_kernel(tc, hidden_states, op_logits, W
                 w_codes[unit] = stream.tile([P, PASSES, N], U32, tag="w_codes", name="w_codes", align_bytes=64)
                 w_scales[unit] = stream.tile([P, PASSES, N], U8, tag="w_scales", name="w_scales", align_bytes=64)
             cut = N - gpsimd_cols(unit, g)
-            nc.vector.quantize_mx(
-                out=w_codes[unit][:, g, 0:cut].bitcast(E4M3X4),
-                scales=w_scales[unit][:, g, 0:cut],
-                in_=staged[(unit, g)][:, 0:cut, :].rearrange("p n t -> p (n t)"),
-            )
             if cut < N:
                 nc.vector.quantize_mx(
                     out=w_codes[unit][:, g, cut:N].bitcast(E4M3X4),
                     scales=w_scales[unit][:, g, cut:N],
                     in_=staged_last[unit][:].rearrange("p n t -> p (n t)"),
                 )
+            nc.vector.quantize_mx(
+                out=w_codes[unit][:, g, 0:cut].bitcast(E4M3X4),
+                scales=w_scales[unit][:, g, 0:cut],
+                in_=staged[(unit, g)][:, 0:cut, :].rearrange("p n t -> p (n t)"),
+            )
 
         acc = {}
         for j in range(TILES):
@@ -335,14 +333,12 @@ def tile_enhancedmathematicalreasoning_pa_kernel(tc, hidden_states, op_logits, W
             now = step - 1
             past = step - 2
             if step < UNITS:
-                for g in range(PASSES):
-                    interleave_on_vector(step, g)
+                interleave_on_vector(step, 0)
             for g in range(PASSES):
                 quantize_w(now, g)
             turned = [read_sum(j) for j in closing_tiles(step)]
             if step < UNITS:
-                if step >= GPSIMD_FROM:
-                    interleave_on_gpsimd(step)
+                interleave_on_gpsimd(step)
                 for g in range(PASSES):
                     interleave_on_scalar(step, g)
             if step in LATE_BIAS_STEPS:

from contextlib import ExitStack

import concourse.mybir as mybir
from concourse.masks import make_identity

TOKENS, H, HO, E = 512, 1024, 1024, 8
FLOPS = 2 * E * TOKENS * H * HO

F32 = mybir.dt.float32
BF16 = mybir.dt.bfloat16
U32 = mybir.dt.uint32
U8 = mybir.dt.uint8
E4M3X4 = mybir.dt.float8_e4m3fn_x4
E5M2X4 = mybir.dt.float8_e5m2_x4
ALU = mybir.AluOpType
ACT = mybir.ActivationFunctionType
AX = mybir.AxisListType

P = 128
PACK = 4
K_PASS = P * PACK
PASSES = H // K_PASS
TILES = TOKENS // P
N = 512
BLOCKS = N // P
HALVES = HO // N
UNITS = HALVES * E
PARTS = 3

SCALAR_TILES = (0,)
VECTOR_TILES = (1, 2, 3)
RING_BANKS = 8 - len(SCALAR_TILES)
STAGE_BUFS = 6
CODE_BUFS = 3
SCALED_BUFS = 2

HEAD_VECTOR_COLS = 448
VECTOR_COLS = 304
COLS_PER_BANK = 64
HEAD_UNITS = 2
GPSIMD_COLS = 256
RUN = 4
LATE_BIAS_STEPS = (3, 4, 5)


def tile_enhancedmathematicalreasoning_pa_kernel(tc, hidden_states, op_logits, We, be, out):
    nc = tc.nc
    x_hbm = hidden_states.rearrange("b s k -> (b s) k").rearrange("(p j) k -> p j k", j=TILES)
    logits_hbm = op_logits.rearrange("b s e -> (b s) e").rearrange("(p j) e -> p j e", j=TILES)
    out_hbm = out.rearrange("b s n -> (b s) n").rearrange("(p j) n -> p j n", j=TILES)

    with ExitStack() as ctx:
        keep = ctx.enter_context(tc.tile_pool(name="keep", bufs=1))
        stream = ctx.enter_context(tc.tile_pool(name="stream", bufs=CODE_BUFS))
        psum = ctx.enter_context(tc.psum_pool(name="psum", bufs=1))
        ctx.enter_context(tc.manual_schedule())

        logits = keep.tile([P, TILES, E], BF16)
        nc.scalar.dma_start(out=logits[:], in_=logits_hbm)
        bias_rows = keep.tile([P, HO], BF16)
        nc.vector.memset(bias_rows[:], 0.0)
        for part in range(PARTS):
            nc.scalar.dma_start(out=bias_rows[part * E : (part + 1) * E, :], in_=be)

        x_raw = {}
        w_raw = {}

        def load_x(j):
            x_raw[j] = keep.tile([P, H], BF16, name="x_raw%d" % j)
            nc.sync.dma_start(out=x_raw[j][:], in_=x_hbm[:, j, :])

        def load_w(unit, g):
            h, e = divmod(unit, E)
            w_raw[(unit, g)] = keep.tile([P, PACK, N], BF16, name="w_raw%d_%d" % (unit, g))
            rows = We[e, g * K_PASS : (g + 1) * K_PASS, h * N : (h + 1) * N]
            nc.sync.dma_start(out=w_raw[(unit, g)][:], in_=rows.rearrange("(p t) n -> p t n", t=PACK))

        load_x(0)
        load_w(0, 0)
        load_x(1)
        load_x(2)
        load_w(0, 1)
        load_x(3)
        for unit in range(1, UNITS):
            for g in range(PASSES):
                load_w(unit, g)

        ident32 = keep.tile([P, P], F32)
        make_identity(nc, ident32[:])
        ident16 = keep.tile([P, P], BF16)
        make_identity(nc, ident16[:])
        parts = keep.tile([P, (TILES - 1) * PARTS * E + P], BF16)
        nc.gpsimd.memset(parts[:], 0.0)

        top = keep.tile([P, TILES], F32)
        nc.vector.tensor_reduce(out=top[:], in_=logits[:], axis=AX.X, op=ALU.max)
        shifted = keep.tile([P, TILES, E], F32)
        nc.vector.tensor_tensor(
            out=shifted[:], in0=logits[:], in1=top[:].unsqueeze(2).to_broadcast([P, TILES, E]), op=ALU.subtract
        )
        exps = keep.tile([P, TILES, E], F32)
        nc.scalar.activation(out=exps[:], in_=shifted[:], func=ACT.Exp)
        total = keep.tile([P, TILES], F32)
        nc.vector.tensor_reduce(out=total[:], in_=exps[:], axis=AX.X, op=ALU.add)
        inverse = keep.tile([P, TILES], F32)
        nc.vector.reciprocal(out=inverse[:], in_=total[:])
        gate = keep.tile([P, TILES, E], F32)
        nc.vector.tensor_tensor(
            out=gate[:], in0=exps[:], in1=inverse[:].unsqueeze(2).to_broadcast([P, TILES, E]), op=ALU.mult
        )

        def ring_bank(shape, dtype):
            return psum.tile(shape, dtype, tag="ring", bufs=RING_BANKS, name="ring")

        x_grouped = {}
        x_codes = {}
        x_scales = {}

        def turn_x(j):
            words = x_raw[j][:].bitcast(F32)
            pass_words = K_PASS // 2
            bank = ring_bank([P, PASSES * 2, P], F32)
            for g in range(PASSES):
                for u in range(2):
                    picked = words[:, g * pass_words + u : (g + 1) * pass_words : 2]
                    nc.tensor.transpose(bank[:, 2 * g + u, :], picked, ident32[:])
            x_grouped[j] = keep.tile([P, PASSES, P, 2], F32, name="x_grouped%d" % j, align_bytes=64)
            nc.scalar.copy(out=x_grouped[j][:], in_=bank[:].rearrange("p (g u) r -> p g r u", u=2))

        def quantize_x(j):
            x_codes[j] = keep.tile([P, PASSES * P], U32, name="x_codes%d" % j, align_bytes=64)
            x_scales[j] = keep.tile([P, PASSES * P], U8, name="x_scales%d" % j, align_bytes=64)
            nc.vector.quantize_mx(
                out=x_codes[j][:].bitcast(E5M2X4),
                scales=x_scales[j][:],
                in_=x_grouped[j][:].rearrange("p g r u -> p (g r u)").bitcast(BF16),
            )

        def scalar_tiles(unit):
            return SCALAR_TILES if unit % E < E - 1 else ()

        def vector_tiles(unit):
            return VECTOR_TILES if unit % E < E - 1 else VECTOR_TILES + SCALAR_TILES

        def closing_tiles(step):
            return SCALAR_TILES if (step - 2) % E == E - 2 else ()

        staged = {}
        w_codes = {}
        w_scales = {}

        def vector_cols(unit, g):
            if unit < HEAD_UNITS:
                return HEAD_VECTOR_COLS
            if g > 0:
                return 0
            scalar_banks = len(scalar_tiles(unit - 1)) + 2 * len(closing_tiles(unit)) + (unit in LATE_BIAS_STEPS)
            return VECTOR_COLS + COLS_PER_BANK * (scalar_banks - len(vector_tiles(unit - 2)))

        def interleave(copy, unit, g, first, last):
            if (unit, g) not in staged:
                staged[(unit, g)] = stream.tile(
                    [P, N, PACK], BF16, tag="staged", name="staged", bufs=STAGE_BUFS, align_bytes=64
                )
            copy(
                out=staged[(unit, g)][:, first:last, :].rearrange("p (c i) t -> p c t i", i=RUN),
                in_=w_raw[(unit, g)][:, :, first:last].rearrange("p t (c i) -> p c t i", i=RUN),
            )

        def interleave_on_vector(unit, g):
            interleave(nc.vector.tensor_copy, unit, g, 0, vector_cols(unit, g))

        def gpsimd_cols(unit, g):
            return GPSIMD_COLS if g == PASSES - 1 and unit >= HEAD_UNITS else 0

        def interleave_on_scalar(unit, g):
            interleave(nc.scalar.copy, unit, g, vector_cols(unit, g), N - gpsimd_cols(unit, g))

        staged_last = {}

        def interleave_on_gpsimd(unit):
            staged_last[unit] = keep.tile(
                [P, GPSIMD_COLS, PACK], BF16, tag="staged_last", name="staged_last", align_bytes=64
            )
            nc.gpsimd.tensor_copy(
                out=staged_last[unit][:],
                in_=w_raw[(unit, PASSES - 1)][:, :, N - GPSIMD_COLS : N].rearrange("p t n -> p n t"),
            )

        def quantize_w(unit, g):
            if g == 0:
                w_codes[unit] = stream.tile([P, PASSES, N], U32, tag="w_codes", name="w_codes", align_bytes=64)
                w_scales[unit] = stream.tile([P, PASSES, N], U8, tag="w_scales", name="w_scales", align_bytes=64)
            cut = N - gpsimd_cols(unit, g)
            if cut < N:
                nc.vector.quantize_mx(
                    out=w_codes[unit][:, g, cut:N].bitcast(E4M3X4),
                    scales=w_scales[unit][:, g, cut:N],
                    in_=staged_last[unit][:].rearrange("p n t -> p (n t)"),
                )
            nc.vector.quantize_mx(
                out=w_codes[unit][:, g, 0:cut].bitcast(E4M3X4),
                scales=w_scales[unit][:, g, 0:cut],
                in_=staged[(unit, g)][:, 0:cut, :].rearrange("p n t -> p (n t)"),
            )

        acc = {}
        for j in range(TILES):
            for h in range(HALVES):
                acc[(j, h)] = keep.tile([P, N], F32, name="acc%d_%d" % (j, h))
        gate_t = keep.tile([P, TILES, P], BF16)
        product = {}
        scaled = {}
        sum_t = {}

        def multiply(unit, j):
            product[(unit, j)] = ring_bank([P, N], F32)
            for g in range(PASSES):
                nc.tensor.matmul_mx(
                    out=product[(unit, j)][:],
                    lhsT=x_codes[j][:, g * P : (g + 1) * P].bitcast(E5M2X4),
                    lhsT_scale=x_scales[j][:, g * P : (g + 1) * P],
                    rhs=w_codes[unit][:, g, :].bitcast(E4M3X4),
                    rhs_scale=w_scales[unit][:, g, :],
                    start=(g == 0),
                    stop=(g == PASSES - 1),
                )

        def gate_column(unit, j):
            return gate[:, j, unit % E : unit % E + 1]

        def scaled_tile():
            return stream.tile([P, N], F32, tag="scaled", name="scaled", bufs=SCALED_BUFS)

        def add_on_vector(unit, j):
            h = unit // E
            nc.vector.scalar_tensor_tensor(
                out=acc[(j, h)][:],
                in0=product[(unit, j)][:],
                scalar=gate_column(unit, j),
                in1=acc[(j, h)][:],
                op0=ALU.mult,
                op1=ALU.add,
            )
            if unit % E == E - 1:
                nc.sync.dma_start(out=out_hbm[:, j, h * N : (h + 1) * N], in_=acc[(j, h)][:])

        def scale_on_scalar(unit, j):
            scaled[(unit, j)] = scaled_tile()
            nc.scalar.activation(
                out=scaled[(unit, j)][:], in_=product[(unit, j)][:], func=ACT.Copy, scale=gate_column(unit, j)
            )

        def bias_term(j, h):
            bank = ring_bank([P, N], F32)
            nc.tensor.matmul(bank[:], lhsT=gate_t[:, j, :], rhs=bias_rows[:, h * N : (h + 1) * N], start=True, stop=True)
            return bank

        def open_sum(j, h):
            sum_t[j] = psum.tile([P, BLOCKS, P], F32, tag="sum_t%d" % j, name="sum_t")
            for b in range(BLOCKS):
                cols = slice(h * N + b * P, h * N + (b + 1) * P)
                nc.tensor.matmul(
                    sum_t[j][:, b, :], lhsT=bias_rows[:, cols], rhs=gate_t[:, j, :], start=(b == 0), stop=False
                )

        def add_transposed(unit, j):
            for b in range(BLOCKS):
                nc.tensor.matmul(
                    sum_t[j][:, b, :],
                    lhsT=scaled[(unit, j)][:, b * P : (b + 1) * P],
                    rhs=ident32[:],
                    is_transpose=True,
                    start=False,
                    stop=(unit % E == E - 2 and b == BLOCKS - 1),
                )

        def read_sum(j):
            turned = scaled_tile()
            nc.scalar.copy(out=turned[:], in_=sum_t[j][:].rearrange("p b r -> p (b r)"))
            return turned

        def turn_back(turned, j, h):
            bank = ring_bank([P, N], F32)
            for b in range(BLOCKS):
                cols = slice(b * P, (b + 1) * P)
                nc.tensor.transpose(bank[:, cols], turned[:, cols], ident32[:])
            nc.scalar.copy(out=acc[(j, h)][:], in_=bank[:])

        part_view = parts[:, 0 : TILES * PARTS * E].rearrange("p (j q e) -> p j q e", q=PARTS, e=E)
        rest = keep.tile([P, TILES, E], F32)
        nc.vector.tensor_copy(out=part_view[:, :, 0, :], in_=gate[:])
        turn_x(0)
        interleave_on_vector(0, 0)
        interleave_on_scalar(0, 0)
        nc.vector.tensor_tensor(out=rest[:], in0=gate[:], in1=part_view[:, :, 0, :], op=ALU.subtract)
        quantize_x(0)
        nc.vector.tensor_copy(out=part_view[:, :, 1, :], in_=rest[:])
        turn_x(1)
        nc.vector.tensor_tensor(out=part_view[:, :, 2, :], in0=rest[:], in1=part_view[:, :, 1, :], op=ALU.subtract)
        quantize_w(0, 0)
        gate_bank = ring_bank([P, TILES, P], BF16)
        for j in range(TILES):
            first = j * PARTS * E
            nc.tensor.transpose(gate_bank[:, j, :], parts[:, first : first + P], ident16[:])
        quantize_x(1)
        interleave_on_vector(0, 1)
        nc.scalar.copy(out=gate_t[:], in_=gate_bank[:])
        turn_x(2)
        interleave_on_scalar(0, 1)
        turn_x(3)
        first_bias = [bias_term(j, 0) for j in VECTOR_TILES]
        quantize_x(2)
        quantize_w(0, 1)
        for j in SCALAR_TILES:
            open_sum(j, 0)
        for j in range(TILES - 1):
            multiply(0, j)
        quantize_x(3)
        for j, bank in zip(VECTOR_TILES, first_bias):
            nc.scalar.copy(out=acc[(j, 0)][:], in_=bank[:])
        multiply(0, TILES - 1)
        for g in range(PASSES):
            interleave_on_vector(1, g)
        for g in range(PASSES):
            interleave_on_scalar(1, g)
        for j in SCALAR_TILES:
            scale_on_scalar(0, j)
        for j in SCALAR_TILES:
            add_transposed(0, j)

        for step in range(2, UNITS + 1):
            now = step - 1
            past = step - 2
            if step < UNITS:
                interleave_on_vector(step, 0)
            for g in range(PASSES):
                quantize_w(now, g)
            turned = [read_sum(j) for j in closing_tiles(step)]
            if step < UNITS:
                interleave_on_gpsimd(step)
                for g in range(PASSES):
                    interleave_on_scalar(step, g)
            if step in LATE_BIAS_STEPS:
                j = VECTOR_TILES[LATE_BIAS_STEPS.index(step)]
                nc.scalar.copy(out=acc[(j, 1)][:], in_=bias_term(j, 1)[:])
            if now % E == 0:
                for j in SCALAR_TILES:
                    open_sum(j, now // E)

            order = scalar_tiles(now) + vector_tiles(now)
            free = min(TILES, RING_BANKS - len(turned) - len(vector_tiles(past)))
            multiply(now, order[0])
            for j, tile_t in zip(closing_tiles(step), turned):
                turn_back(tile_t, j, past // E)
            for j in order[1:free]:
                multiply(now, j)
            for j in vector_tiles(past):
                add_on_vector(past, j)
            for j in order[free:]:
                multiply(now, j)
            for j in scalar_tiles(now):
                scale_on_scalar(now, j)
            for j in scalar_tiles(now):
                add_transposed(now, j)

        for j in vector_tiles(UNITS - 1):
            add_on_vector(UNITS - 1, j)
